import numpy as np
import ml_dtypes


def mxq(x, axis, fmt="e4m3"):
    dtype, down = {"e4m3": (ml_dtypes.float8_e4m3fn, 7), "e5m2": (ml_dtypes.float8_e5m2, 14)}[fmt]
    v = np.moveaxis(np.asarray(x, np.float32).astype(ml_dtypes.bfloat16).astype(np.float64), axis, -1)
    blocks = v.reshape(v.shape[:-1] + (-1, 32))
    amax = np.abs(blocks).max(-1, keepdims=True)
    byte = np.maximum(np.where(amax > 0, np.frexp(amax)[1] - 1 + 127, 0) - down, 1)
    scale = np.exp2(byte - 127.0)
    codes = (blocks / scale).astype(np.float32).astype(dtype).astype(np.float64)
    return np.moveaxis((codes * scale).reshape(v.shape), -1, axis)


WIDE = False


def mx_kscale(k):
    if not WIDE:
        return np.ones(k)
    levels = np.array([10, -10, 5, -5, 0])
    a = np.random.permutation(np.resize(levels, k // 512 * 4)).reshape(k // 512, 4)
    idx = np.arange(k)
    return np.exp2(a[idx // 512, idx % 128 // 32])


BF16 = ml_dtypes.bfloat16


def bf(x):
    return np.asarray(x, np.float32).astype(BF16)


def f64(x):
    return np.asarray(x).astype(np.float64)


E, C, H, I = 2, 256, 512, 8192


def erf(z):
    z = np.clip(z, -6.0, 6.0)
    y = 2.0 * z * z
    acc = np.ones_like(z)
    for n in range(100, 0, -1):
        acc = 1.0 + acc * y / (2 * n + 1)
    return np.clip(2.0 / np.sqrt(np.pi) * z * np.exp(-z * z) * acc, -1.0, 1.0)


def gelu_erf(v):
    return 0.5 * v * (1.0 + erf(v / np.sqrt(2.0)))


def setup_inputs():
    s = mx_kscale(H)
    return {"x": bf(np.random.standard_normal((E * C, H)) * s),
            "w1": bf(np.random.standard_normal((E, H, I)) / np.sqrt(H) / s[:, None]),
            "b1": bf(np.random.standard_normal((E, I)) * 0.3),
            "w2": bf(np.random.standard_normal((E, I, H)) * 1.5 / np.sqrt(I)),
            "b2": bf(np.random.standard_normal((E, H)) * 0.3)}


def reference(x, w1, b1, w2, b2):
    xe = f64(x).reshape(E, C, H)
    h = gelu_erf((mxq(xe, 2, "e4m3") @ mxq(f64(w1), 1, "e4m3")) + f64(b1)[:, None, :])
    out = (mxq(h, 2, "e4m3") @ mxq(f64(w2), 1, "e4m3")) + f64(b2)[:, None, :]
    return out.reshape(E * C, H)

@@ -1,0 +1,188 @@
+from contextlib import ExitStack
+
+import concourse.mybir as mybir
+from concourse.masks import make_identity
+
+BF16 = mybir.dt.bfloat16
+F32 = mybir.dt.float32
+U32 = mybir.dt.uint32
+U8 = mybir.dt.uint8
+FP8X4 = mybir.dt.float8_e4m3fn_x4
+GELU = mybir.ActivationFunctionType.Gelu
+ADD = mybir.AluOpType.add
+
+E, C, H, I = 2, 256, 512, 8192
+P = 128
+PACK = 4
+K_PASS = P * PACK
+UNITS_PER_EXPERT = I // K_PASS
+UNITS = E * UNITS_PER_EXPERT
+TOKEN_TILES = C // P
+WEIGHT_BUFS = 8
+
+FLOPS = 2 * 2 * E * C * H * I
+
+
+def regroup(copy, grouped, rows):
+    copy(
+        out=grouped.rearrange("p (c i) t -> p c t i", i=4),
+        in_=rows.rearrange("p t (c i) -> p c t i", i=4),
+    )
+
+
+def tile_fusedthorexpert_k_kernel(tc, x, w1, b1, w2, b2, out):
+    nc = tc.nc
+    with ExitStack() as ctx:
+        keep = ctx.enter_context(tc.tile_pool(name="keep", bufs=1))
+        weights = ctx.enter_context(tc.tile_pool(name="weights", bufs=WEIGHT_BUFS))
+        work = ctx.enter_context(tc.tile_pool(name="work", bufs=3))
+        banks = ctx.enter_context(tc.psum_pool(name="banks", bufs=4))
+        sums = ctx.enter_context(tc.psum_pool(name="sums", bufs=2))
+
+        def load_w1(u):
+            e, g = divmod(u, UNITS_PER_EXPERT)
+            rows = weights.tile([P, PACK, K_PASS], BF16, name="w1_rows")
+            nc.sync.dma_start(
+                out=rows[:],
+                in_=w1[e, :, K_PASS * g : K_PASS * (g + 1)].rearrange("(t p) i -> p t i", p=P),
+            )
+            return rows
+
+        def load_w2(u):
+            e, g = divmod(u, UNITS_PER_EXPERT)
+            rows = weights.tile([P, PACK, H], BF16, name="w2_rows")
+            nc.sync.dma_start(
+                out=rows[:],
+                in_=w2[e, K_PASS * g : K_PASS * (g + 1), :].rearrange("(t p) n -> p t n", p=P),
+            )
+            return rows
+
+        def quantise(grouped, width, name):
+            codes = work.tile([P, width], U32, align_bytes=64, name=name + "_codes")
+            scales = work.tile([P, width], U8, align_bytes=64, name=name + "_scales")
+            nc.vector.quantize_mx(
+                out=codes[:].bitcast(FP8X4),
+                scales=scales[:],
+                in_=grouped[:].rearrange("p c t -> p (c t)"),
+            )
+            return codes, scales
+
+        x_rows = keep.tile([P, E * TOKEN_TILES, H], BF16)
+        nc.sync.dma_start(out=x_rows[:], in_=x.rearrange("(a p) k -> p a k", p=P))
+        b1_rows = keep.tile([P, P], BF16)
+        nc.sync.dma_start(out=b1_rows[:], in_=b1.rearrange("e (m p) -> (e m) p", p=P))
+        w1_rows = {}
+        w2_rows = {}
+        for u in range(WEIGHT_BUFS):
+            w1_rows[u] = load_w1(u)
+            w2_rows[u] = load_w2(u)
+        b2_all = keep.tile([P, E, H], BF16)
+        nc.sync.dma_start(
+            out=b2_all[:].rearrange("p e n -> p (e n)"),
+            in_=b2.rearrange("e n -> (e n)").partition_broadcast(P),
+        )
+
+        warm = keep.tile([P, 1], F32)
+        nc.vector.memset(warm[:], 0.0)
+        nc.scalar.activation(out=warm[:], in_=warm[:], func=GELU)
+
+        ident = keep.tile([P, P], BF16)
+        make_identity(nc, ident[:])
+        x_grouped = keep.tile([P, E * C, PACK], BF16, align_bytes=64)
+        for a in range(E * TOKEN_TILES):
+            x_t = banks.tile([P, PACK, P], BF16, tag="bank")
+            for t in range(PACK):
+                nc.tensor.transpose(x_t[:, t, :], x_rows[:, a, P * t : P * (t + 1)], ident[:])
+            nc.vector.tensor_copy(
+                out=x_grouped[:, P * a : P * (a + 1), :], in_=x_t[:].rearrange("p t r -> p r t")
+            )
+        x_codes = keep.tile([P, E * C], U32, align_bytes=64)
+        x_scales = keep.tile([P, E * C], U8, align_bytes=64)
+        nc.vector.quantize_mx(
+            out=x_codes[:].bitcast(FP8X4),
+            scales=x_scales[:],
+            in_=x_grouped[:].rearrange("p r t -> p (r t)"),
+        )
+
+        b1_t = banks.tile([P, P], BF16, tag="bank")
+        nc.tensor.transpose(b1_t[:], b1_rows[:], ident[:])
+        b1_cols = keep.tile([P, P], F32)
+        nc.vector.tensor_copy(out=b1_cols[:], in_=b1_t[:])
+
+        w1_grouped = {}
+        h_rows = {}
+        acc = {}
+
+        def regroup_w1(u):
+            w1_grouped[u] = work.tile([P, K_PASS, PACK], BF16, align_bytes=64, name="w1_grouped")
+            regroup(nc.scalar.copy, w1_grouped[u][:], w1_rows[u][:])
+            if u + WEIGHT_BUFS < UNITS:
+                w1_rows[u + WEIGHT_BUFS] = load_w1(u + WEIGHT_BUFS)
+
+        def first_matmul_and_gelu(u):
+            e = u // UNITS_PER_EXPERT
+            w1_codes, w1_scales = quantise(w1_grouped[u], K_PASS, "w1")
+            tokens = slice(C * e, C * (e + 1))
+            h_rows[u] = work.tile([P, PACK, C], BF16, name="h_rows")
+            for half in range(PACK // 2):
+                h_sums = banks.tile([P, 2, C], F32, tag="bank")
+                for s in range(2):
+                    t = 2 * half + s
+                    nc.tensor.matmul_mx(
+                        out=h_sums[:, s, :],
+                        lhsT=w1_codes[:, P * t : P * (t + 1)].bitcast(FP8X4),
+                        lhsT_scale=w1_scales[:, P * t : P * (t + 1)],
+                        rhs=x_codes[:, tokens].bitcast(FP8X4),
+                        rhs_scale=x_scales[:, tokens],
+                        start=True,
+                        stop=True,
+                    )
+                for s in range(2):
+                    t = 2 * half + s
+                    m = PACK * u + t
+                    nc.scalar.activation(
+                        out=h_rows[u][:, t, :],
+                        in_=h_sums[:, s, :],
+                        func=GELU,
+                        bias=b1_cols[:, m : m + 1],
+                    )
+
+        def second_matmul(u):
+            e, g = divmod(u, UNITS_PER_EXPERT)
+            h_grouped = work.tile([P, C, PACK], BF16, align_bytes=64)
+            regroup(nc.vector.tensor_copy, h_grouped[:], h_rows[u][:])
+            w2_grouped = work.tile([P, H, PACK], BF16, align_bytes=64)
+            regroup(nc.vector.tensor_copy, w2_grouped[:], w2_rows[u][:])
+            if u + WEIGHT_BUFS < UNITS:
+                w2_rows[u + WEIGHT_BUFS] = load_w2(u + WEIGHT_BUFS)
+            h_codes, h_scales = quantise(h_grouped, C, "h")
+            w2_codes, w2_scales = quantise(w2_grouped, H, "w2")
+            for c in range(TOKEN_TILES):
+                if g == 0:
+                    acc[c] = sums.tile([P, H], F32, name="acc%d" % c)
+                nc.tensor.matmul_mx(
+                    out=acc[c][:],
+                    lhsT=h_codes[:, P * c : P * (c + 1)].bitcast(FP8X4),
+                    lhsT_scale=h_scales[:, P * c : P * (c + 1)],
+                    rhs=w2_codes[:].bitcast(FP8X4),
+                    rhs_scale=w2_scales[:],
+                    start=(g == 0),
+                    stop=(g == UNITS_PER_EXPERT - 1),
+                )
+            if g == UNITS_PER_EXPERT - 1:
+                for c in range(TOKEN_TILES):
+                    result = work.tile([P, H], F32)
+                    nc.vector.tensor_tensor(
+                        out=result[:], in0=acc[c][:], in1=b2_all[:, e, :], op=ADD
+                    )
+                    first = C * e + P * c
+                    nc.sync.dma_start(out=out[first : first + P, :], in_=result[:])
+
+        regroup_w1(0)
+        for u in range(UNITS + 1):
+            if u + 1 < UNITS:
+                regroup_w1(u + 1)
+            if u < UNITS:
+                first_matmul_and_gelu(u)
+            if u > 0:
+                second_matmul(u - 1)

@@ -38,6 +38,7 @@ def tile_fusedthorexpert_k_kernel(tc, x, w1, b1, w2, b2, out):
         work = ctx.enter_context(tc.tile_pool(name="work", bufs=3))
         banks = ctx.enter_context(tc.psum_pool(name="banks", bufs=4))
         sums = ctx.enter_context(tc.psum_pool(name="sums", bufs=2))
+        ctx.enter_context(tc.manual_schedule())
 
         def load_w1(u):
             e, g = divmod(u, UNITS_PER_EXPERT)

@@ -19,6 +19,7 @@ UNITS_PER_EXPERT = I // K_PASS
 UNITS = E * UNITS_PER_EXPERT
 TOKEN_TILES = C // P
 WEIGHT_BUFS = 8
+VECTOR_W1_PERIOD = 16
 
 FLOPS = 2 * 2 * E * C * H * I
 
@@ -68,20 +69,18 @@ def tile_fusedthorexpert_k_kernel(tc, x, w1, b1, w2, b2, out):
             )
             return codes, scales
 
+        w1_rows = {}
+        w2_rows = {}
+        w1_rows[0] = load_w1(0)
         x_rows = keep.tile([P, E * TOKEN_TILES, H], BF16)
         nc.sync.dma_start(out=x_rows[:], in_=x.rearrange("(a p) k -> p a k", p=P))
         b1_rows = keep.tile([P, P], BF16)
         nc.sync.dma_start(out=b1_rows[:], in_=b1.rearrange("e (m p) -> (e m) p", p=P))
-        w1_rows = {}
-        w2_rows = {}
-        for u in range(WEIGHT_BUFS):
+        for u in range(1, WEIGHT_BUFS):
             w1_rows[u] = load_w1(u)
-            w2_rows[u] = load_w2(u)
+            w2_rows[u - 1] = load_w2(u - 1)
+        w2_rows[WEIGHT_BUFS - 1] = load_w2(WEIGHT_BUFS - 1)
         b2_all = keep.tile([P, E, H], BF16)
-        nc.sync.dma_start(
-            out=b2_all[:].rearrange("p e n -> p (e n)"),
-            in_=b2.rearrange("e n -> (e n)").partition_broadcast(P),
-        )
 
         warm = keep.tile([P, 1], F32)
         nc.vector.memset(warm[:], 0.0)
@@ -111,53 +110,65 @@ def tile_fusedthorexpert_k_kernel(tc, x, w1, b1, w2, b2, out):
         nc.vector.tensor_copy(out=b1_cols[:], in_=b1_t[:])
 
         w1_grouped = {}
+        h_sums = {}
         h_rows = {}
+        h_grouped = {}
+        w2_grouped = {}
+        w2_quantised = {}
         acc = {}
 
         def regroup_w1(u):
             w1_grouped[u] = work.tile([P, K_PASS, PACK], BF16, align_bytes=64, name="w1_grouped")
-            regroup(nc.scalar.copy, w1_grouped[u][:], w1_rows[u][:])
+            if u % VECTOR_W1_PERIOD == VECTOR_W1_PERIOD // 2:
+                regroup(nc.vector.tensor_copy, w1_grouped[u][:], w1_rows[u][:])
+            else:
+                regroup(nc.scalar.copy, w1_grouped[u][:], w1_rows[u][:])
             if u + WEIGHT_BUFS < UNITS:
                 w1_rows[u + WEIGHT_BUFS] = load_w1(u + WEIGHT_BUFS)
 
-        def first_matmul_and_gelu(u):
-            e = u // UNITS_PER_EXPERT
+        def first_matmul(u):
             w1_codes, w1_scales = quantise(w1_grouped[u], K_PASS, "w1")
+            e = u // UNITS_PER_EXPERT
             tokens = slice(C * e, C * (e + 1))
+            for t in range(PACK):
+                if t % 2 == 0:
+                    bank = banks.tile([P, 2, C], F32, tag="bank")
+                h_sums[u, t] = bank[:, t % 2, :]
+                nc.tensor.matmul_mx(
+                    out=h_sums[u, t],
+                    lhsT=w1_codes[:, P * t : P * (t + 1)].bitcast(FP8X4),
+                    lhsT_scale=w1_scales[:, P * t : P * (t + 1)],
+                    rhs=x_codes[:, tokens].bitcast(FP8X4),
+                    rhs_scale=x_scales[:, tokens],
+                    start=True,
+                    stop=True,
+                )
+
+        def gelu(u):
             h_rows[u] = work.tile([P, PACK, C], BF16, name="h_rows")
-            for half in range(PACK // 2):
-                h_sums = banks.tile([P, 2, C], F32, tag="bank")
-                for s in range(2):
-                    t = 2 * half + s
-                    nc.tensor.matmul_mx(
-                        out=h_sums[:, s, :],
-                        lhsT=w1_codes[:, P * t : P * (t + 1)].bitcast(FP8X4),
-                        lhsT_scale=w1_scales[:, P * t : P * (t + 1)],
-                        rhs=x_codes[:, tokens].bitcast(FP8X4),
-                        rhs_scale=x_scales[:, tokens],
-                        start=True,
-                        stop=True,
-                    )
-                for s in range(2):
-                    t = 2 * half + s
-                    m = PACK * u + t
-                    nc.scalar.activation(
-                        out=h_rows[u][:, t, :],
-                        in_=h_sums[:, s, :],
-                        func=GELU,
-                        bias=b1_cols[:, m : m + 1],
-                    )
+            for t in range(PACK):
+                m = PACK * u + t
+                nc.scalar.activation(
+                    out=h_rows[u][:, t, :], in_=h_sums[u, t], func=GELU, bias=b1_cols[:, m : m + 1]
+                )
+
+        def regroup_w2(u):
+            w2_grouped[u] = work.tile([P, H, PACK], BF16, align_bytes=64, name="w2_grouped")
+            regroup(nc.vector.tensor_copy, w2_grouped[u][:], w2_rows[u][:])
+            if u + WEIGHT_BUFS < UNITS:
+                w2_rows[u + WEIGHT_BUFS] = load_w2(u + WEIGHT_BUFS)
+
+        def regroup_h(u):
+            h_grouped[u] = work.tile([P, C, PACK], BF16, align_bytes=64, name="h_grouped")
+            regroup(nc.vector.tensor_copy, h_grouped[u][:], h_rows[u][:])
+
+        def quantise_w2(u):
+            w2_quantised[u] = quantise(w2_grouped[u], H, "w2")
 
         def second_matmul(u):
             e, g = divmod(u, UNITS_PER_EXPERT)
-            h_grouped = work.tile([P, C, PACK], BF16, align_bytes=64)
-            regroup(nc.vector.tensor_copy, h_grouped[:], h_rows[u][:])
-            w2_grouped = work.tile([P, H, PACK], BF16, align_bytes=64)
-            regroup(nc.vector.tensor_copy, w2_grouped[:], w2_rows[u][:])
-            if u + WEIGHT_BUFS < UNITS:
-                w2_rows[u + WEIGHT_BUFS] = load_w2(u + WEIGHT_BUFS)
-            h_codes, h_scales = quantise(h_grouped, C, "h")
-            w2_codes, w2_scales = quantise(w2_grouped, H, "w2")
+            h_codes, h_scales = quantise(h_grouped[u], C, "h")
+            w2_codes, w2_scales = w2_quantised[u]
             for c in range(TOKEN_TILES):
                 if g == 0:
                     acc[c] = sums.tile([P, H], F32, name="acc%d" % c)
@@ -179,11 +190,25 @@ def tile_fusedthorexpert_k_kernel(tc, x, w1, b1, w2, b2, out):
                     first = C * e + P * c
                     nc.sync.dma_start(out=out[first : first + P, :], in_=result[:])
 
-        regroup_w1(0)
-        for u in range(UNITS + 1):
-            if u + 1 < UNITS:
-                regroup_w1(u + 1)
-            if u < UNITS:
-                first_matmul_and_gelu(u)
-            if u > 0:
-                second_matmul(u - 1)
+        def live(u):
+            return 0 <= u < UNITS
+
+        for step in range(UNITS + 3):
+            if live(step):
+                regroup_w1(step)
+            if step == UNITS_PER_EXPERT // 2:
+                nc.sync.dma_start(
+                    out=b2_all[:].rearrange("p e n -> p (e n)"),
+                    in_=b2.rearrange("e n -> (e n)").partition_broadcast(P),
+                )
+            if live(step - 1):
+                first_matmul(step - 1)
+            if live(step - 2):
+                gelu(step - 2)
+                regroup_w2(step - 2)
+            if live(step - 3):
+                regroup_h(step - 3)
+            if live(step - 2):
+                quantise_w2(step - 2)
+            if live(step - 3):
+                second_matmul(step - 3)

@@ -19,7 +19,8 @@ UNITS_PER_EXPERT = I // K_PASS
 UNITS = E * UNITS_PER_EXPERT
 TOKEN_TILES = C // P
 WEIGHT_BUFS = 8
-VECTOR_W1_PERIOD = 16
+MOVED = 192
+MATMUL_COLS = 512
 
 FLOPS = 2 * 2 * E * C * H * I
 
@@ -38,7 +39,8 @@ def tile_fusedthorexpert_k_kernel(tc, x, w1, b1, w2, b2, out):
         weights = ctx.enter_context(tc.tile_pool(name="weights", bufs=WEIGHT_BUFS))
         work = ctx.enter_context(tc.tile_pool(name="work", bufs=3))
         banks = ctx.enter_context(tc.psum_pool(name="banks", bufs=4))
-        sums = ctx.enter_context(tc.psum_pool(name="sums", bufs=2))
+        moves = ctx.enter_context(tc.psum_pool(name="moves", bufs=2))
+        sums = ctx.enter_context(tc.psum_pool(name="sums", bufs=1))
         ctx.enter_context(tc.manual_schedule())
 
         def load_w1(u):
@@ -109,6 +111,7 @@ def tile_fusedthorexpert_k_kernel(tc, x, w1, b1, w2, b2, out):
         b1_cols = keep.tile([P, P], F32)
         nc.vector.tensor_copy(out=b1_cols[:], in_=b1_t[:])
 
+        w1_moved = {}
         w1_grouped = {}
         h_sums = {}
         h_rows = {}
@@ -117,12 +120,24 @@ def tile_fusedthorexpert_k_kernel(tc, x, w1, b1, w2, b2, out):
         w2_quantised = {}
         acc = {}
 
+        def move_w1(u):
+            w1_moved[u] = moves.tile([P, MOVED, PACK], BF16, name="w1_moved")
+            for c in range(0, MOVED, MATMUL_COLS // PACK):
+                cols = slice(c, min(c + MATMUL_COLS // PACK, MOVED))
+                rows = slice(K_PASS - MOVED + cols.start, K_PASS - MOVED + cols.stop)
+                nc.tensor.matmul(
+                    out=w1_moved[u][:, cols, :],
+                    lhsT=ident[:],
+                    rhs=w1_rows[u][:, :, rows].rearrange("p t c -> p c t"),
+                    start=True,
+                    stop=True,
+                )
+
         def regroup_w1(u):
             w1_grouped[u] = work.tile([P, K_PASS, PACK], BF16, align_bytes=64, name="w1_grouped")
-            if u % VECTOR_W1_PERIOD == VECTOR_W1_PERIOD // 2:
-                regroup(nc.vector.tensor_copy, w1_grouped[u][:], w1_rows[u][:])
-            else:
-                regroup(nc.scalar.copy, w1_grouped[u][:], w1_rows[u][:])
+            direct = K_PASS - MOVED
+            regroup(nc.scalar.copy, w1_grouped[u][:, :direct, :], w1_rows[u][:, :, :direct])
+            nc.scalar.copy(out=w1_grouped[u][:, direct:, :], in_=w1_moved[u][:])
             if u + WEIGHT_BUFS < UNITS:
                 w1_rows[u + WEIGHT_BUFS] = load_w1(u + WEIGHT_BUFS)
 
@@ -193,7 +208,10 @@ def tile_fusedthorexpert_k_kernel(tc, x, w1, b1, w2, b2, out):
         def live(u):
             return 0 <= u < UNITS
 
+        move_w1(0)
         for step in range(UNITS + 3):
+            if live(step + 1):
+                move_w1(step + 1)
             if live(step):
                 regroup_w1(step)
             if step == UNITS_PER_EXPERT // 2:

@@ -20,6 +20,7 @@ UNITS = E * UNITS_PER_EXPERT
 TOKEN_TILES = C // P
 WEIGHT_BUFS = 8
 MOVED = 192
+RUN = 8
 MATMUL_COLS = 512
 
 FLOPS = 2 * 2 * E * C * H * I
@@ -27,8 +28,8 @@ FLOPS = 2 * 2 * E * C * H * I
 
 def regroup(copy, grouped, rows):
     copy(
-        out=grouped.rearrange("p (c i) t -> p c t i", i=4),
-        in_=rows.rearrange("p t (c i) -> p c t i", i=4),
+        out=grouped.rearrange("p (c i) t -> p c t i", i=RUN),
+        in_=rows.rearrange("p t (c i) -> p c t i", i=RUN),
     )
 
 

@@ -21,6 +21,7 @@ TOKEN_TILES = C // P
 WEIGHT_BUFS = 8
 MOVED = 192
 RUN = 8
+W2_ON_SCALAR = 64
 MATMUL_COLS = 512
 
 FLOPS = 2 * 2 * E * C * H * I
@@ -38,7 +39,7 @@ def tile_fusedthorexpert_k_kernel(tc, x, w1, b1, w2, b2, out):
     with ExitStack() as ctx:
         keep = ctx.enter_context(tc.tile_pool(name="keep", bufs=1))
         weights = ctx.enter_context(tc.tile_pool(name="weights", bufs=WEIGHT_BUFS))
-        work = ctx.enter_context(tc.tile_pool(name="work", bufs=3))
+        work = ctx.enter_context(tc.tile_pool(name="work", bufs=4))
         banks = ctx.enter_context(tc.psum_pool(name="banks", bufs=4))
         moves = ctx.enter_context(tc.psum_pool(name="moves", bufs=2))
         sums = ctx.enter_context(tc.psum_pool(name="sums", bufs=1))
@@ -168,9 +169,14 @@ def tile_fusedthorexpert_k_kernel(tc, x, w1, b1, w2, b2, out):
                     out=h_rows[u][:, t, :], in_=h_sums[u, t], func=GELU, bias=b1_cols[:, m : m + 1]
                 )
 
-        def regroup_w2(u):
+        def regroup_w2_on_scalar(u):
             w2_grouped[u] = work.tile([P, H, PACK], BF16, align_bytes=64, name="w2_grouped")
-            regroup(nc.vector.tensor_copy, w2_grouped[u][:], w2_rows[u][:])
+            cols = slice(H - W2_ON_SCALAR, H)
+            regroup(nc.scalar.copy, w2_grouped[u][:, cols, :], w2_rows[u][:, :, cols])
+
+        def regroup_w2(u):
+            cols = slice(0, H - W2_ON_SCALAR)
+            regroup(nc.vector.tensor_copy, w2_grouped[u][:, cols, :], w2_rows[u][:, :, cols])
             if u + WEIGHT_BUFS < UNITS:
                 w2_rows[u + WEIGHT_BUFS] = load_w2(u + WEIGHT_BUFS)
 
@@ -221,6 +227,7 @@ def tile_fusedthorexpert_k_kernel(tc, x, w1, b1, w2, b2, out):
                     in_=b2.rearrange("e n -> (e n)").partition_broadcast(P),
                 )
             if live(step - 1):
+                regroup_w2_on_scalar(step - 1)
                 first_matmul(step - 1)
             if live(step - 2):
                 gelu(step - 2)

@@ -19,9 +19,10 @@ UNITS_PER_EXPERT = I // K_PASS
 UNITS = E * UNITS_PER_EXPERT
 TOKEN_TILES = C // P
 WEIGHT_BUFS = 8
+FIRST_ON_VECTOR = 256
 MOVED = 192
 RUN = 8
-W2_ON_SCALAR = 64
+W2_ON_SCALAR = 48
 MATMUL_COLS = 512
 
 FLOPS = 2 * 2 * E * C * H * I
@@ -50,7 +51,7 @@ def tile_fusedthorexpert_k_kernel(tc, x, w1, b1, w2, b2, out):
             rows = weights.tile([P, PACK, K_PASS], BF16, name="w1_rows")
             nc.sync.dma_start(
                 out=rows[:],
-                in_=w1[e, :, K_PASS * g : K_PASS * (g + 1)].rearrange("(t p) i -> p t i", p=P),
+                in_=w1[e, :, K_PASS * g : K_PASS * (g + 1)].rearrange("(p t) i -> p t i", p=P),
             )
             return rows
 
@@ -75,14 +76,25 @@ def tile_fusedthorexpert_k_kernel(tc, x, w1, b1, w2, b2, out):
 
         w1_rows = {}
         w2_rows = {}
+        x_rows = {}
+        x_codes = {}
+        x_scales = {}
+
+        def load_x(e):
+            x_rows[e] = keep.tile([P, TOKEN_TILES, H], BF16, name="x_rows%d" % e)
+            nc.sync.dma_start(
+                out=x_rows[e][:], in_=x[C * e : C * (e + 1), :].rearrange("(a p) k -> p a k", p=P)
+            )
+
         w1_rows[0] = load_w1(0)
-        x_rows = keep.tile([P, E * TOKEN_TILES, H], BF16)
-        nc.sync.dma_start(out=x_rows[:], in_=x.rearrange("(a p) k -> p a k", p=P))
+        load_x(0)
         b1_rows = keep.tile([P, P], BF16)
         nc.sync.dma_start(out=b1_rows[:], in_=b1.rearrange("e (m p) -> (e m) p", p=P))
         for u in range(1, WEIGHT_BUFS):
             w1_rows[u] = load_w1(u)
             w2_rows[u - 1] = load_w2(u - 1)
+            if u == WEIGHT_BUFS // 2:
+                load_x(1)
         w2_rows[WEIGHT_BUFS - 1] = load_w2(WEIGHT_BUFS - 1)
         b2_all = keep.tile([P, E, H], BF16)
 
@@ -92,26 +104,37 @@ def tile_fusedthorexpert_k_kernel(tc, x, w1, b1, w2, b2, out):
 
         ident = keep.tile([P, P], BF16)
         make_identity(nc, ident[:])
-        x_grouped = keep.tile([P, E * C, PACK], BF16, align_bytes=64)
-        for a in range(E * TOKEN_TILES):
-            x_t = banks.tile([P, PACK, P], BF16, tag="bank")
-            for t in range(PACK):
-                nc.tensor.transpose(x_t[:, t, :], x_rows[:, a, P * t : P * (t + 1)], ident[:])
-            nc.vector.tensor_copy(
-                out=x_grouped[:, P * a : P * (a + 1), :], in_=x_t[:].rearrange("p t r -> p r t")
-            )
-        x_codes = keep.tile([P, E * C], U32, align_bytes=64)
-        x_scales = keep.tile([P, E * C], U8, align_bytes=64)
-        nc.vector.quantize_mx(
-            out=x_codes[:].bitcast(FP8X4),
-            scales=x_scales[:],
-            in_=x_grouped[:].rearrange("p r t -> p (r t)"),
-        )
+        ident_words = keep.tile([P, P], F32)
+        make_identity(nc, ident_words[:])
 
-        b1_t = banks.tile([P, P], BF16, tag="bank")
-        nc.tensor.transpose(b1_t[:], b1_rows[:], ident[:])
+        x_banks = {}
+        x_grouped = {}
+
+        def transpose_x(e):
+            x_banks[e] = banks.tile([P, TOKEN_TILES, 2, P], F32, tag="bank", name="x_bank")
+            for a in range(TOKEN_TILES):
+                words = x_rows[e][:, a, :].bitcast(F32)
+                for j in range(2):
+                    nc.tensor.transpose(x_banks[e][:, a, j, :], words[:, j::2], ident_words[:])
+
+        def regroup_x(e):
+            x_grouped[e] = keep.tile([P, C * PACK], BF16, align_bytes=64, name="x_grouped%d" % e)
+            nc.vector.tensor_copy(
+                out=x_grouped[e][:].bitcast(F32).rearrange(
+                    "p (a r j) -> p a r j", a=TOKEN_TILES, j=2
+                ),
+                in_=x_banks[e][:].rearrange("p a j r -> p a r j"),
+            )
+
+        def quantise_x(e):
+            x_codes[e] = keep.tile([P, C], U32, align_bytes=64, name="x_codes%d" % e)
+            x_scales[e] = keep.tile([P, C], U8, align_bytes=64, name="x_scales%d" % e)
+            nc.vector.quantize_mx(
+                out=x_codes[e][:].bitcast(FP8X4), scales=x_scales[e][:], in_=x_grouped[e][:]
+            )
+
         b1_cols = keep.tile([P, P], F32)
-        nc.vector.tensor_copy(out=b1_cols[:], in_=b1_t[:])
+        b1_t = banks.tile([P, P], BF16, tag="bank")
 
         w1_moved = {}
         w1_grouped = {}
@@ -137,16 +160,21 @@ def tile_fusedthorexpert_k_kernel(tc, x, w1, b1, w2, b2, out):
 
         def regroup_w1(u):
             w1_grouped[u] = work.tile([P, K_PASS, PACK], BF16, align_bytes=64, name="w1_grouped")
-            direct = K_PASS - MOVED
-            regroup(nc.scalar.copy, w1_grouped[u][:, :direct, :], w1_rows[u][:, :, :direct])
-            nc.scalar.copy(out=w1_grouped[u][:, direct:, :], in_=w1_moved[u][:])
+            if u == 0:
+                mine = slice(0, FIRST_ON_VECTOR)
+                rest = slice(FIRST_ON_VECTOR, K_PASS)
+                regroup(nc.vector.tensor_copy, w1_grouped[u][:, mine, :], w1_rows[u][:, :, mine])
+                regroup(nc.scalar.copy, w1_grouped[u][:, rest, :], w1_rows[u][:, :, rest])
+            else:
+                direct = K_PASS - MOVED
+                regroup(nc.scalar.copy, w1_grouped[u][:, :direct, :], w1_rows[u][:, :, :direct])
+                nc.scalar.copy(out=w1_grouped[u][:, direct:, :], in_=w1_moved[u][:])
             if u + WEIGHT_BUFS < UNITS:
                 w1_rows[u + WEIGHT_BUFS] = load_w1(u + WEIGHT_BUFS)
 
         def first_matmul(u):
             w1_codes, w1_scales = quantise(w1_grouped[u], K_PASS, "w1")
             e = u // UNITS_PER_EXPERT
-            tokens = slice(C * e, C * (e + 1))
             for t in range(PACK):
                 if t % 2 == 0:
                     bank = banks.tile([P, 2, C], F32, tag="bank")
@@ -155,8 +183,8 @@ def tile_fusedthorexpert_k_kernel(tc, x, w1, b1, w2, b2, out):
                     out=h_sums[u, t],
                     lhsT=w1_codes[:, P * t : P * (t + 1)].bitcast(FP8X4),
                     lhsT_scale=w1_scales[:, P * t : P * (t + 1)],
-                    rhs=x_codes[:, tokens].bitcast(FP8X4),
-                    rhs_scale=x_scales[:, tokens],
+                    rhs=x_codes[e][:].bitcast(FP8X4),
+                    rhs_scale=x_scales[e][:],
                     start=True,
                     stop=True,
                 )
@@ -215,26 +243,36 @@ def tile_fusedthorexpert_k_kernel(tc, x, w1, b1, w2, b2, out):
         def live(u):
             return 0 <= u < UNITS
 
-        move_w1(0)
+        transpose_x(0)
+        nc.tensor.transpose(b1_t[:], b1_rows[:], ident[:])
         for step in range(UNITS + 3):
             if live(step + 1):
                 move_w1(step + 1)
             if live(step):
                 regroup_w1(step)
+            if step == 0:
+                regroup_x(0)
+                nc.vector.tensor_copy(out=b1_cols[:], in_=b1_t[:])
+                quantise_x(0)
             if step == UNITS_PER_EXPERT // 2:
+                transpose_x(1)
                 nc.sync.dma_start(
                     out=b2_all[:].rearrange("p e n -> p (e n)"),
                     in_=b2.rearrange("e n -> (e n)").partition_broadcast(P),
                 )
             if live(step - 1):
                 regroup_w2_on_scalar(step - 1)
+                regroup_w2(step - 1)
                 first_matmul(step - 1)
             if live(step - 2):
                 gelu(step - 2)
-                regroup_w2(step - 2)
             if live(step - 3):
                 regroup_h(step - 3)
-            if live(step - 2):
-                quantise_w2(step - 2)
+            if step == UNITS_PER_EXPERT // 2:
+                regroup_x(1)
+            if live(step - 1):
+                quantise_w2(step - 1)
+            if step == UNITS_PER_EXPERT // 2:
+                quantise_x(1)
             if live(step - 3):
                 second_matmul(step - 3)

@@ -20,7 +20,7 @@ UNITS = E * UNITS_PER_EXPERT
 TOKEN_TILES = C // P
 WEIGHT_BUFS = 8
 FIRST_ON_VECTOR = 256
-MOVED = 192
+MOVED = 200
 RUN = 8
 W2_ON_SCALAR = 48
 MATMUL_COLS = 512
@@ -189,56 +189,70 @@ def tile_fusedthorexpert_k_kernel(tc, x, w1, b1, w2, b2, out):
                     stop=True,
                 )
 
+        def token_pieces(u):
+            width = P if u == UNITS - 1 else C
+            return [slice(c, c + width) for c in range(0, C, width)]
+
         def gelu(u):
             h_rows[u] = work.tile([P, PACK, C], BF16, name="h_rows")
-            for t in range(PACK):
-                m = PACK * u + t
-                nc.scalar.activation(
-                    out=h_rows[u][:, t, :], in_=h_sums[u, t], func=GELU, bias=b1_cols[:, m : m + 1]
-                )
+            for tokens in token_pieces(u):
+                for t in range(PACK):
+                    m = PACK * u + t
+                    nc.scalar.activation(
+                        out=h_rows[u][:, t, tokens],
+                        in_=h_sums[u, t][:, tokens],
+                        func=GELU,
+                        bias=b1_cols[:, m : m + 1],
+                    )
+
+        def w2_on_vector(u):
+            return 0 if u == UNITS - 1 else H - W2_ON_SCALAR
 
         def regroup_w2_on_scalar(u):
             w2_grouped[u] = work.tile([P, H, PACK], BF16, align_bytes=64, name="w2_grouped")
-            cols = slice(H - W2_ON_SCALAR, H)
+            cols = slice(w2_on_vector(u), H)
             regroup(nc.scalar.copy, w2_grouped[u][:, cols, :], w2_rows[u][:, :, cols])
 
         def regroup_w2(u):
-            cols = slice(0, H - W2_ON_SCALAR)
-            regroup(nc.vector.tensor_copy, w2_grouped[u][:, cols, :], w2_rows[u][:, :, cols])
+            if w2_on_vector(u) > 0:
+                cols = slice(0, w2_on_vector(u))
+                regroup(nc.vector.tensor_copy, w2_grouped[u][:, cols, :], w2_rows[u][:, :, cols])
             if u + WEIGHT_BUFS < UNITS:
                 w2_rows[u + WEIGHT_BUFS] = load_w2(u + WEIGHT_BUFS)
 
-        def regroup_h(u):
-            h_grouped[u] = work.tile([P, C, PACK], BF16, align_bytes=64, name="h_grouped")
-            regroup(nc.vector.tensor_copy, h_grouped[u][:], h_rows[u][:])
+        def regroup_h(u, tokens):
+            if tokens.start == 0:
+                h_grouped[u] = work.tile([P, C, PACK], BF16, align_bytes=64, name="h_grouped")
+            regroup(nc.vector.tensor_copy, h_grouped[u][:, tokens, :], h_rows[u][:, :, tokens])
 
         def quantise_w2(u):
             w2_quantised[u] = quantise(w2_grouped[u], H, "w2")
 
-        def second_matmul(u):
-            e, g = divmod(u, UNITS_PER_EXPERT)
-            h_codes, h_scales = quantise(h_grouped[u], C, "h")
+        def second_matmul(u, tokens):
+            g = u % UNITS_PER_EXPERT
+            width = tokens.stop - tokens.start
+            h_codes, h_scales = quantise(h_grouped[u][:, tokens, :], width, "h")
             w2_codes, w2_scales = w2_quantised[u]
-            for c in range(TOKEN_TILES):
+            for c in range(0, width, P):
+                tile = (tokens.start + c) // P
                 if g == 0:
-                    acc[c] = sums.tile([P, H], F32, name="acc%d" % c)
+                    acc[tile] = sums.tile([P, H], F32, name="acc%d" % tile)
                 nc.tensor.matmul_mx(
-                    out=acc[c][:],
-                    lhsT=h_codes[:, P * c : P * (c + 1)].bitcast(FP8X4),
-                    lhsT_scale=h_scales[:, P * c : P * (c + 1)],
+                    out=acc[tile][:],
+                    lhsT=h_codes[:, c : c + P].bitcast(FP8X4),
+                    lhsT_scale=h_scales[:, c : c + P],
                     rhs=w2_codes[:].bitcast(FP8X4),
                     rhs_scale=w2_scales[:],
                     start=(g == 0),
                     stop=(g == UNITS_PER_EXPERT - 1),
                 )
-            if g == UNITS_PER_EXPERT - 1:
-                for c in range(TOKEN_TILES):
-                    result = work.tile([P, H], F32)
-                    nc.vector.tensor_tensor(
-                        out=result[:], in0=acc[c][:], in1=b2_all[:, e, :], op=ADD
-                    )
-                    first = C * e + P * c
-                    nc.sync.dma_start(out=out[first : first + P, :], in_=result[:])
+
+        def finish(e):
+            for c in range(TOKEN_TILES):
+                result = work.tile([P, H], F32)
+                nc.vector.tensor_tensor(out=result[:], in0=acc[c][:], in1=b2_all[:, e, :], op=ADD)
+                first = C * e + P * c
+                nc.sync.dma_start(out=out[first : first + P, :], in_=result[:])
 
         def live(u):
             return 0 <= u < UNITS
@@ -266,13 +280,19 @@ def tile_fusedthorexpert_k_kernel(tc, x, w1, b1, w2, b2, out):
                 first_matmul(step - 1)
             if live(step - 2):
                 gelu(step - 2)
-            if live(step - 3):
-                regroup_h(step - 3)
-            if step == UNITS_PER_EXPERT // 2:
-                regroup_x(1)
-            if live(step - 1):
-                quantise_w2(step - 1)
-            if step == UNITS_PER_EXPERT // 2:
-                quantise_x(1)
-            if live(step - 3):
-                second_matmul(step - 3)
+            for tokens in token_pieces(step - 3):
+                if live(step - 3):
+                    regroup_h(step - 3, tokens)
+                if step == UNITS_PER_EXPERT // 2:
+                    regroup_x(1)
+                if step == UNITS_PER_EXPERT + 3:
+                    finish(0)
+                if live(step - 1) and step - 1 != UNITS - 1:
+                    quantise_w2(step - 1)
+                if step - 2 == UNITS - 1:
+                    quantise_w2(step - 2)
+                if step == UNITS_PER_EXPERT // 2:
+                    quantise_x(1)
+                if live(step - 3):
+                    second_matmul(step - 3, tokens)
+        finish(E - 1)

@@ -20,9 +20,10 @@ UNITS = E * UNITS_PER_EXPERT
 TOKEN_TILES = C // P
 WEIGHT_BUFS = 8
 FIRST_ON_VECTOR = 256
-MOVED = 200
+MOVED = 208
 RUN = 8
-W2_ON_SCALAR = 48
+W2_ON_SCALAR = (48, 64)
+STORE_COLS = H // 2
 MATMUL_COLS = 512
 
 FLOPS = 2 * 2 * E * C * H * I
@@ -196,7 +197,7 @@ def tile_fusedthorexpert_k_kernel(tc, x, w1, b1, w2, b2, out):
         def gelu(u):
             h_rows[u] = work.tile([P, PACK, C], BF16, name="h_rows")
             for tokens in token_pieces(u):
-                for t in range(PACK):
+                for t in reversed(range(PACK)):
                     m = PACK * u + t
                     nc.scalar.activation(
                         out=h_rows[u][:, t, tokens],
@@ -206,12 +207,15 @@ def tile_fusedthorexpert_k_kernel(tc, x, w1, b1, w2, b2, out):
                     )
 
         def w2_on_vector(u):
-            return 0 if u == UNITS - 1 else H - W2_ON_SCALAR
+            if u == 0:
+                return H
+            return 0 if u == UNITS - 1 else H - W2_ON_SCALAR[u % 2]
 
         def regroup_w2_on_scalar(u):
             w2_grouped[u] = work.tile([P, H, PACK], BF16, align_bytes=64, name="w2_grouped")
-            cols = slice(w2_on_vector(u), H)
-            regroup(nc.scalar.copy, w2_grouped[u][:, cols, :], w2_rows[u][:, :, cols])
+            if w2_on_vector(u) < H:
+                cols = slice(w2_on_vector(u), H)
+                regroup(nc.scalar.copy, w2_grouped[u][:, cols, :], w2_rows[u][:, :, cols])
 
         def regroup_w2(u):
             if w2_on_vector(u) > 0:
@@ -249,10 +253,14 @@ def tile_fusedthorexpert_k_kernel(tc, x, w1, b1, w2, b2, out):
 
         def finish(e):
             for c in range(TOKEN_TILES):
-                result = work.tile([P, H], F32)
-                nc.vector.tensor_tensor(out=result[:], in0=acc[c][:], in1=b2_all[:, e, :], op=ADD)
                 first = C * e + P * c
-                nc.sync.dma_start(out=out[first : first + P, :], in_=result[:])
+                for n in range(0, H, STORE_COLS):
+                    cols = slice(n, n + STORE_COLS)
+                    result = work.tile([P, STORE_COLS], F32)
+                    nc.vector.tensor_tensor(
+                        out=result[:], in0=acc[c][:, cols], in1=b2_all[:, e, cols], op=ADD
+                    )
+                    nc.sync.dma_start(out=out[first : first + P, cols], in_=result[:])
 
         def live(u):
             return 0 <= u < UNITS

@@ -19,7 +19,7 @@ UNITS_PER_EXPERT = I // K_PASS
 UNITS = E * UNITS_PER_EXPERT
 TOKEN_TILES = C // P
 WEIGHT_BUFS = 8
-FIRST_ON_VECTOR = 256
+W1_ON_VECTOR = (256, 128, 128, 128)
 MOVED = 208
 RUN = 8
 W2_ON_SCALAR = (48, 64)
@@ -161,15 +161,13 @@ def tile_fusedthorexpert_k_kernel(tc, x, w1, b1, w2, b2, out):
 
         def regroup_w1(u):
             w1_grouped[u] = work.tile([P, K_PASS, PACK], BF16, align_bytes=64, name="w1_grouped")
-            if u == 0:
-                mine = slice(0, FIRST_ON_VECTOR)
-                rest = slice(FIRST_ON_VECTOR, K_PASS)
-                regroup(nc.vector.tensor_copy, w1_grouped[u][:, mine, :], w1_rows[u][:, :, mine])
-                regroup(nc.scalar.copy, w1_grouped[u][:, rest, :], w1_rows[u][:, :, rest])
-            else:
-                direct = K_PASS - MOVED
-                regroup(nc.scalar.copy, w1_grouped[u][:, :direct, :], w1_rows[u][:, :, :direct])
-                nc.scalar.copy(out=w1_grouped[u][:, direct:, :], in_=w1_moved[u][:])
+            start = W1_ON_VECTOR[u] if u < len(W1_ON_VECTOR) else 0
+            stop = K_PASS - MOVED if u > 0 else K_PASS
+            if start > 0:
+                regroup(nc.vector.tensor_copy, w1_grouped[u][:, :start, :], w1_rows[u][:, :, :start])
+            regroup(nc.scalar.copy, w1_grouped[u][:, start:stop, :], w1_rows[u][:, :, start:stop])
+            if stop < K_PASS:
+                nc.scalar.copy(out=w1_grouped[u][:, stop:, :], in_=w1_moved[u][:])
             if u + WEIGHT_BUFS < UNITS:
                 w1_rows[u + WEIGHT_BUFS] = load_w1(u + WEIGHT_BUFS)
 

from contextlib import ExitStack

import concourse.mybir as mybir
from concourse.masks import make_identity

BF16 = mybir.dt.bfloat16
F32 = mybir.dt.float32
U32 = mybir.dt.uint32
U8 = mybir.dt.uint8
FP8X4 = mybir.dt.float8_e4m3fn_x4
GELU = mybir.ActivationFunctionType.Gelu
ADD = mybir.AluOpType.add

E, C, H, I = 2, 256, 512, 8192
P = 128
PACK = 4
K_PASS = P * PACK
UNITS_PER_EXPERT = I // K_PASS
UNITS = E * UNITS_PER_EXPERT
TOKEN_TILES = C // P
WEIGHT_BUFS = 8
W1_ON_VECTOR = (256, 128, 128, 128)
MOVED = 208
RUN = 8
W2_ON_SCALAR = (48, 64)
STORE_COLS = H // 2
MATMUL_COLS = 512

FLOPS = 2 * 2 * E * C * H * I


def regroup(copy, grouped, rows):
    copy(
        out=grouped.rearrange("p (c i) t -> p c t i", i=RUN),
        in_=rows.rearrange("p t (c i) -> p c t i", i=RUN),
    )


def tile_fusedthorexpert_k_kernel(tc, x, w1, b1, w2, b2, out):
    nc = tc.nc
    with ExitStack() as ctx:
        keep = ctx.enter_context(tc.tile_pool(name="keep", bufs=1))
        weights = ctx.enter_context(tc.tile_pool(name="weights", bufs=WEIGHT_BUFS))
        work = ctx.enter_context(tc.tile_pool(name="work", bufs=4))
        banks = ctx.enter_context(tc.psum_pool(name="banks", bufs=4))
        moves = ctx.enter_context(tc.psum_pool(name="moves", bufs=2))
        sums = ctx.enter_context(tc.psum_pool(name="sums", bufs=1))
        ctx.enter_context(tc.manual_schedule())

        def load_w1(u):
            e, g = divmod(u, UNITS_PER_EXPERT)
            rows = weights.tile([P, PACK, K_PASS], BF16, name="w1_rows")
            nc.sync.dma_start(
                out=rows[:],
                in_=w1[e, :, K_PASS * g : K_PASS * (g + 1)].rearrange("(p t) i -> p t i", p=P),
            )
            return rows

        def load_w2(u):
            e, g = divmod(u, UNITS_PER_EXPERT)
            rows = weights.tile([P, PACK, H], BF16, name="w2_rows")
            nc.sync.dma_start(
                out=rows[:],
                in_=w2[e, K_PASS * g : K_PASS * (g + 1), :].rearrange("(t p) n -> p t n", p=P),
            )
            return rows

        def quantise(grouped, width, name):
            codes = work.tile([P, width], U32, align_bytes=64, name=name + "_codes")
            scales = work.tile([P, width], U8, align_bytes=64, name=name + "_scales")
            nc.vector.quantize_mx(
                out=codes[:].bitcast(FP8X4),
                scales=scales[:],
                in_=grouped[:].rearrange("p c t -> p (c t)"),
            )
            return codes, scales

        w1_rows = {}
        w2_rows = {}
        x_rows = {}
        x_codes = {}
        x_scales = {}

        def load_x(e):
            x_rows[e] = keep.tile([P, TOKEN_TILES, H], BF16, name="x_rows%d" % e)
            nc.sync.dma_start(
                out=x_rows[e][:], in_=x[C * e : C * (e + 1), :].rearrange("(a p) k -> p a k", p=P)
            )

        w1_rows[0] = load_w1(0)
        load_x(0)
        b1_rows = keep.tile([P, P], BF16)
        nc.sync.dma_start(out=b1_rows[:], in_=b1.rearrange("e (m p) -> (e m) p", p=P))
        for u in range(1, WEIGHT_BUFS):
            w1_rows[u] = load_w1(u)
            w2_rows[u - 1] = load_w2(u - 1)
            if u == WEIGHT_BUFS // 2:
                load_x(1)
        w2_rows[WEIGHT_BUFS - 1] = load_w2(WEIGHT_BUFS - 1)
        b2_all = keep.tile([P, E, H], BF16)

        warm = keep.tile([P, 1], F32)
        nc.vector.memset(warm[:], 0.0)
        nc.scalar.activation(out=warm[:], in_=warm[:], func=GELU)

        ident = keep.tile([P, P], BF16)
        make_identity(nc, ident[:])
        ident_words = keep.tile([P, P], F32)
        make_identity(nc, ident_words[:])

        x_banks = {}
        x_grouped = {}

        def transpose_x(e):
            x_banks[e] = banks.tile([P, TOKEN_TILES, 2, P], F32, tag="bank", name="x_bank")
            for a in range(TOKEN_TILES):
                words = x_rows[e][:, a, :].bitcast(F32)
                for j in range(2):
                    nc.tensor.transpose(x_banks[e][:, a, j, :], words[:, j::2], ident_words[:])

        def regroup_x(e):
            x_grouped[e] = keep.tile([P, C * PACK], BF16, align_bytes=64, name="x_grouped%d" % e)
            nc.vector.tensor_copy(
                out=x_grouped[e][:].bitcast(F32).rearrange(
                    "p (a r j) -> p a r j", a=TOKEN_TILES, j=2
                ),
                in_=x_banks[e][:].rearrange("p a j r -> p a r j"),
            )

        def quantise_x(e):
            x_codes[e] = keep.tile([P, C], U32, align_bytes=64, name="x_codes%d" % e)
            x_scales[e] = keep.tile([P, C], U8, align_bytes=64, name="x_scales%d" % e)
            nc.vector.quantize_mx(
                out=x_codes[e][:].bitcast(FP8X4), scales=x_scales[e][:], in_=x_grouped[e][:]
            )

        b1_cols = keep.tile([P, P], F32)
        b1_t = banks.tile([P, P], BF16, tag="bank")

        w1_moved = {}
        w1_grouped = {}
        h_sums = {}
        h_rows = {}
        h_grouped = {}
        w2_grouped = {}
        w2_quantised = {}
        acc = {}

        def move_w1(u):
            w1_moved[u] = moves.tile([P, MOVED, PACK], BF16, name="w1_moved")
            for c in range(0, MOVED, MATMUL_COLS // PACK):
                cols = slice(c, min(c + MATMUL_COLS // PACK, MOVED))
                rows = slice(K_PASS - MOVED + cols.start, K_PASS - MOVED + cols.stop)
                nc.tensor.matmul(
                    out=w1_moved[u][:, cols, :],
                    lhsT=ident[:],
                    rhs=w1_rows[u][:, :, rows].rearrange("p t c -> p c t"),
                    start=True,
                    stop=True,
                )

        def regroup_w1(u):
            w1_grouped[u] = work.tile([P, K_PASS, PACK], BF16, align_bytes=64, name="w1_grouped")
            start = W1_ON_VECTOR[u] if u < len(W1_ON_VECTOR) else 0
            stop = K_PASS - MOVED if u > 0 else K_PASS
            if start > 0:
                regroup(nc.vector.tensor_copy, w1_grouped[u][:, :start, :], w1_rows[u][:, :, :start])
            regroup(nc.scalar.copy, w1_grouped[u][:, start:stop, :], w1_rows[u][:, :, start:stop])
            if stop < K_PASS:
                nc.scalar.copy(out=w1_grouped[u][:, stop:, :], in_=w1_moved[u][:])
            if u + WEIGHT_BUFS < UNITS:
                w1_rows[u + WEIGHT_BUFS] = load_w1(u + WEIGHT_BUFS)

        def first_matmul(u):
            w1_codes, w1_scales = quantise(w1_grouped[u], K_PASS, "w1")
            e = u // UNITS_PER_EXPERT
            for t in range(PACK):
                if t % 2 == 0:
                    bank = banks.tile([P, 2, C], F32, tag="bank")
                h_sums[u, t] = bank[:, t % 2, :]
                nc.tensor.matmul_mx(
                    out=h_sums[u, t],
                    lhsT=w1_codes[:, P * t : P * (t + 1)].bitcast(FP8X4),
                    lhsT_scale=w1_scales[:, P * t : P * (t + 1)],
                    rhs=x_codes[e][:].bitcast(FP8X4),
                    rhs_scale=x_scales[e][:],
                    start=True,
                    stop=True,
                )

        def token_pieces(u):
            width = P if u == UNITS - 1 else C
            return [slice(c, c + width) for c in range(0, C, width)]

        def gelu(u):
            h_rows[u] = work.tile([P, PACK, C], BF16, name="h_rows")
            for tokens in token_pieces(u):
                for t in reversed(range(PACK)):
                    m = PACK * u + t
                    nc.scalar.activation(
                        out=h_rows[u][:, t, tokens],
                        in_=h_sums[u, t][:, tokens],
                        func=GELU,
                        bias=b1_cols[:, m : m + 1],
                    )

        def w2_on_vector(u):
            if u == 0:
                return H
            return 0 if u == UNITS - 1 else H - W2_ON_SCALAR[u % 2]

        def regroup_w2_on_scalar(u):
            w2_grouped[u] = work.tile([P, H, PACK], BF16, align_bytes=64, name="w2_grouped")
            if w2_on_vector(u) < H:
                cols = slice(w2_on_vector(u), H)
                regroup(nc.scalar.copy, w2_grouped[u][:, cols, :], w2_rows[u][:, :, cols])

        def regroup_w2(u):
            if w2_on_vector(u) > 0:
                cols = slice(0, w2_on_vector(u))
                regroup(nc.vector.tensor_copy, w2_grouped[u][:, cols, :], w2_rows[u][:, :, cols])
            if u + WEIGHT_BUFS < UNITS:
                w2_rows[u + WEIGHT_BUFS] = load_w2(u + WEIGHT_BUFS)

        def regroup_h(u, tokens):
            if tokens.start == 0:
                h_grouped[u] = work.tile([P, C, PACK], BF16, align_bytes=64, name="h_grouped")
            regroup(nc.vector.tensor_copy, h_grouped[u][:, tokens, :], h_rows[u][:, :, tokens])

        def quantise_w2(u):
            w2_quantised[u] = quantise(w2_grouped[u], H, "w2")

        def second_matmul(u, tokens):
            g = u % UNITS_PER_EXPERT
            width = tokens.stop - tokens.start
            h_codes, h_scales = quantise(h_grouped[u][:, tokens, :], width, "h")
            w2_codes, w2_scales = w2_quantised[u]
            for c in range(0, width, P):
                tile = (tokens.start + c) // P
                if g == 0:
                    acc[tile] = sums.tile([P, H], F32, name="acc%d" % tile)
                nc.tensor.matmul_mx(
                    out=acc[tile][:],
                    lhsT=h_codes[:, c : c + P].bitcast(FP8X4),
                    lhsT_scale=h_scales[:, c : c + P],
                    rhs=w2_codes[:].bitcast(FP8X4),
                    rhs_scale=w2_scales[:],
                    start=(g == 0),
                    stop=(g == UNITS_PER_EXPERT - 1),
                )

        def finish(e):
            for c in range(TOKEN_TILES):
                first = C * e + P * c
                for n in range(0, H, STORE_COLS):
                    cols = slice(n, n + STORE_COLS)
                    result = work.tile([P, STORE_COLS], F32)
                    nc.vector.tensor_tensor(
                        out=result[:], in0=acc[c][:, cols], in1=b2_all[:, e, cols], op=ADD
                    )
                    nc.sync.dma_start(out=out[first : first + P, cols], in_=result[:])

        def live(u):
            return 0 <= u < UNITS

        transpose_x(0)
        nc.tensor.transpose(b1_t[:], b1_rows[:], ident[:])
        for step in range(UNITS + 3):
            if live(step + 1):
                move_w1(step + 1)
            if live(step):
                regroup_w1(step)
            if step == 0:
                regroup_x(0)
                nc.vector.tensor_copy(out=b1_cols[:], in_=b1_t[:])
                quantise_x(0)
            if step == UNITS_PER_EXPERT // 2:
                transpose_x(1)
                nc.sync.dma_start(
                    out=b2_all[:].rearrange("p e n -> p (e n)"),
                    in_=b2.rearrange("e n -> (e n)").partition_broadcast(P),
                )
            if live(step - 1):
                regroup_w2_on_scalar(step - 1)
                regroup_w2(step - 1)
                first_matmul(step - 1)
            if live(step - 2):
                gelu(step - 2)
            for tokens in token_pieces(step - 3):
                if live(step - 3):
                    regroup_h(step - 3, tokens)
                if step == UNITS_PER_EXPERT // 2:
                    regroup_x(1)
                if step == UNITS_PER_EXPERT + 3:
                    finish(0)
                if live(step - 1) and step - 1 != UNITS - 1:
                    quantise_w2(step - 1)
                if step - 2 == UNITS - 1:
                    quantise_w2(step - 2)
                if step == UNITS_PER_EXPERT // 2:
                    quantise_x(1)
                if live(step - 3):
                    second_matmul(step - 3, tokens)
        finish(E - 1)
